import numpy as np
import ml_dtypes


def mxq(x, axis, fmt="e4m3"):
    dtype, down = {"e4m3": (ml_dtypes.float8_e4m3fn, 7), "e5m2": (ml_dtypes.float8_e5m2, 14)}[fmt]
    v = np.moveaxis(np.asarray(x, np.float32).astype(ml_dtypes.bfloat16).astype(np.float64), axis, -1)
    blocks = v.reshape(v.shape[:-1] + (-1, 32))
    amax = np.abs(blocks).max(-1, keepdims=True)
    byte = np.maximum(np.where(amax > 0, np.frexp(amax)[1] - 1 + 127, 0) - down, 1)
    scale = np.exp2(byte - 127.0)
    codes = (blocks / scale).astype(np.float32).astype(dtype).astype(np.float64)
    return np.moveaxis((codes * scale).reshape(v.shape), -1, axis)


WIDE = False


def mx_kscale(k):
    if not WIDE:
        return np.ones(k)
    levels = np.array([10, -10, 5, -5, 0])
    a = np.random.permutation(np.resize(levels, k // 512 * 4)).reshape(k // 512, 4)
    idx = np.arange(k)
    return np.exp2(a[idx // 512, idx % 128 // 32])


BF16 = ml_dtypes.bfloat16


def bf(x):
    return np.asarray(x, np.float32).astype(BF16)


def f64(x):
    return np.asarray(x).astype(np.float64)


B, N, F, O, E, K = 16, 512, 256, 64, 16, 3


def normalize_adj(a):
    a = np.maximum(a, 0.0) + np.eye(N)[None, :, :]
    d = np.maximum(a.sum(-1), 1e-6)
    r = d ** -0.5
    return r[:, :, None] * a * r[:, None, :]


def setup_inputs():
    s = mx_kscale(N)
    u = (s / s.min()) ** 2
    x = 0.7 * np.random.standard_normal((B, N, F)) + 0.7 * np.random.standard_normal((B, 1, F))
    x = x * (s / s.max())[None, :, None]
    a0 = 0.5 * (np.random.standard_normal((B, N, N)) - 1.0)
    a = u[None, :, None] * a0
    i = np.arange(N)
    a[:, i, i] = u[None, :] * (np.maximum(a0[:, i, i], 0.0) + 1.0) - 1.0
    return {"A": bf(a), "x": bf(x)}


def reference(A, x):
    a_hat = normalize_adj(f64(A))
    a_left = mxq(a_hat, 2, "e4m3")
    xq = mxq(f64(x), 1, "e4m3")
    t2 = 2.0 * (a_left @ mxq(a_hat, 1, "e4m3")) - np.eye(N)[None, :, :]
    xg1 = a_left @ xq
    xg2 = mxq(t2, 2, "e4m3") @ xq
    return np.stack([xg1, xg2], axis=1)

@@ -1,0 +1,255 @@
+from contextlib import ExitStack
+
+import concourse.mybir as mybir
+from concourse.masks import make_identity
+
+F32 = mybir.dt.float32
+BF16 = mybir.dt.bfloat16
+U32 = mybir.dt.uint32
+U8 = mybir.dt.uint8
+FP8X4 = mybir.dt.float8_e4m3fn_x4
+ALU = mybir.AluOpType
+ACT = mybir.ActivationFunctionType
+
+GRAPHS = 16
+NODES = 512
+FEATS = 256
+P = 128
+PACK = 4
+
+LOADS_AHEAD = 4
+
+FLOPS = GRAPHS * 2 * (NODES * NODES * NODES + 2 * NODES * NODES * FEATS)
+
+
+def rows_by_node(dram):
+    return dram.rearrange("(u p e) w -> p u (e w)", u=2, e=2)
+
+
+def slots_by_node(tile):
+    return tile[:].rearrange("p (u e) w -> p u (e w)", u=2)
+
+
+def quantise(nc, pool, grouped, width, name):
+    codes = pool.tile([P, width], U32, align_bytes=64, name=name + "_codes")
+    scales = pool.tile([P, width], U8, align_bytes=64, name=name + "_scales")
+    nc.vector.quantize_mx(out=codes[:].bitcast(FP8X4), scales=scales[:], in_=grouped)
+    return codes, scales
+
+
+def tile_dygcn_pa_t_kernel(tc, A, x, out):
+    nc = tc.nc
+    with ExitStack() as stack:
+        const = stack.enter_context(tc.tile_pool(name="const", bufs=1))
+        loads = stack.enter_context(tc.tile_pool(name="loads", bufs=LOADS_AHEAD + 2))
+        work = stack.enter_context(tc.tile_pool(name="work", bufs=2))
+        small = stack.enter_context(tc.tile_pool(name="small", bufs=3))
+        mx = stack.enter_context(tc.tile_pool(name="mx", bufs=3))
+        results = stack.enter_context(tc.tile_pool(name="results", bufs=4))
+        ps_row = stack.enter_context(tc.psum_pool(name="ps_row", bufs=1))
+        ps_tr = stack.enter_context(tc.psum_pool(name="ps_tr", bufs=2))
+        ps_t2 = stack.enter_context(tc.psum_pool(name="ps_t2", bufs=3))
+        ps_out = stack.enter_context(tc.psum_pool(name="ps_out", bufs=2))
+
+        ident_f32 = const.tile([P, P], F32)
+        make_identity(nc, ident_f32[:])
+        eye_t2 = const.tile([P, PACK, P, PACK], BF16)
+        nc.vector.memset(eye_t2[:], 0.0)
+        for c in range(PACK):
+            nc.vector.tensor_copy(out=eye_t2[:, c, :, c], in_=ident_f32[:])
+
+        live = {}
+
+        def load(b):
+            a_raw = loads.tile([P, PACK, NODES], BF16)
+            nc.sync.dma_start(out=slots_by_node(a_raw), in_=rows_by_node(A[b]))
+            x_raw = loads.tile([P, PACK, FEATS], BF16)
+            nc.sync.dma_start(out=slots_by_node(x_raw), in_=rows_by_node(x[b]))
+            live["a_raw", b] = a_raw
+            live["x_raw", b] = x_raw
+
+        def positive_part(b):
+            a_raw = live["a_raw", b]
+            pos = work.tile([P, PACK, NODES], F32)
+            rowsum = small.tile([P, PACK], F32)
+            for t in range(PACK):
+                nc.scalar.activation(
+                    out=pos[:, t, :], in_=a_raw[:, t, :], func=ACT.Relu, accum_out=rowsum[:, t : t + 1]
+                )
+            for t in range(PACK):
+                diag = pos[:, t, :].rearrange("p (u q e) -> p u q e", u=2, e=2)[:, t // 2, :, t % 2]
+                nc.gpsimd.tensor_tensor(out=diag, in0=diag, in1=ident_f32[:], op=ALU.add)
+            live["pos", b] = pos
+            live["rowsum", b] = rowsum
+
+        def inverse_root(b):
+            deg = small.tile([P, PACK], F32)
+            nc.vector.tensor_scalar(
+                out=deg[:], in0=live["rowsum", b][:], scalar1=1.0, scalar2=1e-6, op0=ALU.add, op1=ALU.max
+            )
+            inv_deg = small.tile([P, PACK], F32)
+            nc.vector.reciprocal(out=inv_deg[:], in_=deg[:])
+            r = small.tile([P, PACK], F32)
+            nc.scalar.activation(out=r[:], in_=inv_deg[:], func=ACT.Sqrt)
+            live["r", b] = r
+
+        def spread_r(b):
+            r = live["r", b]
+            r_row = ps_row.tile([P, NODES], F32)
+            for t in range(PACK):
+                nc.tensor.transpose(
+                    r_row[:].rearrange("p (u q e) -> p u q e", u=2, e=2)[:, t // 2, :, t % 2],
+                    r[:, t : t + 1].to_broadcast([P, P]),
+                    ident_f32[:],
+                )
+            live["r_row", b] = r_row
+
+        def scale(b):
+            a_hat = work.tile([P, PACK, NODES], BF16)
+            for t in range(PACK):
+                nc.vector.scalar_tensor_tensor(
+                    out=a_hat[:, t, :],
+                    in0=live["pos", b][:, t, :],
+                    scalar=live["r", b][:, t : t + 1],
+                    in1=live["r_row", b][:],
+                    op0=ALU.mult,
+                    op1=ALU.mult,
+                )
+            live["a_hat", b] = a_hat
+
+        def regroup_right(b):
+            right_grouped = work.tile([P, NODES * PACK], BF16, align_bytes=64)
+            right_words = right_grouped[:].rearrange("p (t q s) -> p t q s", t=PACK, s=PACK)
+            columns = live["a_hat", b][:].rearrange("p s (u q e) -> p u e q s", u=2, e=2)
+            for t in range(PACK):
+                copy = nc.scalar.copy if t == PACK - 1 else nc.vector.tensor_copy
+                copy(out=right_words[:, t, :, :], in_=columns[:, t // 2, t % 2, :, :])
+            live["right_grouped", b] = right_grouped
+
+        def flip(b):
+            for h in range(2):
+                flipped = ps_tr.tile([P, 2, 2, P], F32)
+                for c in range(2):
+                    row_words = live["a_hat", b][:, 2 * h + c, :].bitcast(F32)
+                    for u in range(2):
+                        nc.tensor.transpose(flipped[:, c, u, :], row_words[:, u * P : (u + 1) * P], ident_f32[:])
+                live["flipped", b, h] = flipped
+
+        def regroup_left(b):
+            left_grouped = work.tile([P, NODES * PACK], BF16, align_bytes=64)
+            left_words = left_grouped[:].bitcast(F32).rearrange("p (h c n u) -> p h c n u", h=2, c=2, u=2)
+            for h in range(2):
+                nc.scalar.copy(
+                    out=left_words[:, h, :, :, :], in_=live["flipped", b, h][:].rearrange("p c u n -> p c n u")
+                )
+            live["left_grouped", b] = left_grouped
+
+        def regroup_x(b):
+            x_grouped = work.tile([P, FEATS * PACK], BF16, align_bytes=64)
+            nc.scalar.copy(
+                out=x_grouped[:].rearrange("p (f s) -> p f s", s=PACK),
+                in_=live["x_raw", b][:].rearrange("p s f -> p f s"),
+            )
+            live["x_grouped", b] = x_grouped
+
+        def square(b, c):
+            right_codes, right_scales = live["right", b]
+            left_codes, left_scales = live["left", b]
+            n_cols = slice(c * P, (c + 1) * P)
+            squared = ps_t2.tile([P, PACK, P], F32)
+            for t in range(PACK):
+                j_cols = slice(t * P, (t + 1) * P)
+                nc.tensor.matmul_mx(
+                    out=squared[:, t, :],
+                    lhsT=right_codes[:, j_cols].bitcast(FP8X4),
+                    lhsT_scale=right_scales[:, j_cols],
+                    rhs=left_codes[:, n_cols].bitcast(FP8X4),
+                    rhs_scale=left_scales[:, n_cols],
+                    start=True,
+                    stop=True,
+                )
+            live["squared", b, c] = squared
+
+        def chebyshev(b, c):
+            if c == 0:
+                live["t2_grouped", b] = work.tile([P, NODES * PACK], BF16, align_bytes=64, name="t2_grouped")
+            nc.vector.scalar_tensor_tensor(
+                out=live["t2_grouped", b][:].rearrange("p (c n t) -> p c n t", c=PACK, t=PACK)[:, c, :, :],
+                in0=live["squared", b, c][:].rearrange("p t n -> p n t"),
+                scalar=2.0,
+                in1=eye_t2[:, c, :, :],
+                op0=ALU.mult,
+                op1=ALU.subtract,
+            )
+
+        def times_x(b, name):
+            codes, scales = live[name, b]
+            x_codes, x_scales = live["x", b]
+            for h in range(2):
+                acc = ps_out.tile([P, 2, FEATS], F32)
+                for c in range(2):
+                    n_cols = slice((2 * h + c) * P, (2 * h + c + 1) * P)
+                    nc.tensor.matmul_mx(
+                        out=acc[:, c, :],
+                        lhsT=codes[:, n_cols].bitcast(FP8X4),
+                        lhsT_scale=scales[:, n_cols],
+                        rhs=x_codes[:].bitcast(FP8X4),
+                        rhs_scale=x_scales[:],
+                        start=True,
+                        stop=True,
+                    )
+                live["acc", b, h] = acc
+
+        def store(b, which):
+            result = results.tile([P, PACK, FEATS], F32)
+            for h in range(2):
+                nc.scalar.copy(out=result[:, 2 * h : 2 * h + 2, :], in_=live["acc", b, h][:])
+            nc.sync.dma_start(out=rows_by_node(out[b, which]), in_=slots_by_node(result))
+
+        def quantise_as(b, name, width):
+            live[name, b] = quantise(nc, mx, live[name + "_grouped", b][:], width, name)
+
+        with tc.manual_schedule():
+            for b in range(LOADS_AHEAD):
+                load(b)
+            for i in range(-2, GRAPHS + 1):
+                front, middle, back, last = i + 2, i + 1, i, i - 1
+                if front + LOADS_AHEAD < GRAPHS:
+                    load(front + LOADS_AHEAD)
+                if 0 <= last:
+                    times_x(last, "t2")
+                if 0 <= middle < GRAPHS:
+                    scale(middle)
+                if front < GRAPHS:
+                    positive_part(front)
+                if 0 <= back < GRAPHS:
+                    for c in range(PACK - 1):
+                        square(back, c)
+                if 0 <= last:
+                    store(last, 1)
+                if 0 <= middle < GRAPHS:
+                    flip(middle)
+                if 0 <= back < GRAPHS:
+                    for c in range(PACK - 1):
+                        chebyshev(back, c)
+                    square(back, PACK - 1)
+                    chebyshev(back, PACK - 1)
+                if 0 <= middle < GRAPHS:
+                    regroup_left(middle)
+                if front < GRAPHS:
+                    inverse_root(front)
+                if 0 <= back < GRAPHS:
+                    times_x(back, "left")
+                if front < GRAPHS:
+                    spread_r(front)
+                if 0 <= middle < GRAPHS:
+                    regroup_right(middle)
+                if 0 <= back < GRAPHS:
+                    store(back, 0)
+                    quantise_as(back, "t2", NODES)
+                if 0 <= middle < GRAPHS:
+                    quantise_as(middle, "x", FEATS)
+                    quantise_as(middle, "left", NODES)
+                    quantise_as(middle, "right", NODES)
+                if front < GRAPHS:
+                    regroup_x(front)

@@ -42,8 +42,9 @@ def tile_dygcn_pa_t_kernel(tc, A, x, out):
     with ExitStack() as stack:
         const = stack.enter_context(tc.tile_pool(name="const", bufs=1))
         loads = stack.enter_context(tc.tile_pool(name="loads", bufs=LOADS_AHEAD + 2))
+        early = stack.enter_context(tc.tile_pool(name="early", bufs=3))
         work = stack.enter_context(tc.tile_pool(name="work", bufs=2))
-        small = stack.enter_context(tc.tile_pool(name="small", bufs=3))
+        small = stack.enter_context(tc.tile_pool(name="small", bufs=4))
         mx = stack.enter_context(tc.tile_pool(name="mx", bufs=3))
         results = stack.enter_context(tc.tile_pool(name="results", bufs=4))
         ps_row = stack.enter_context(tc.psum_pool(name="ps_row", bufs=1))
@@ -70,17 +71,19 @@ def tile_dygcn_pa_t_kernel(tc, A, x, out):
 
         def positive_part(b):
             a_raw = live["a_raw", b]
-            pos = work.tile([P, PACK, NODES], F32)
+            pos = early.tile([P, PACK, NODES], F32)
             rowsum = small.tile([P, PACK], F32)
             for t in range(PACK):
                 nc.scalar.activation(
                     out=pos[:, t, :], in_=a_raw[:, t, :], func=ACT.Relu, accum_out=rowsum[:, t : t + 1]
                 )
-            for t in range(PACK):
-                diag = pos[:, t, :].rearrange("p (u q e) -> p u q e", u=2, e=2)[:, t // 2, :, t % 2]
-                nc.gpsimd.tensor_tensor(out=diag, in0=diag, in1=ident_f32[:], op=ALU.add)
             live["pos", b] = pos
             live["rowsum", b] = rowsum
+
+        def add_identity(b):
+            for t in range(PACK):
+                diag = live["pos", b][:, t, :].rearrange("p (u q e) -> p u q e", u=2, e=2)[:, t // 2, :, t % 2]
+                nc.gpsimd.tensor_tensor(out=diag, in0=diag, in1=ident_f32[:], op=ALU.add)
 
         def inverse_root(b):
             deg = small.tile([P, PACK], F32)
@@ -121,9 +124,15 @@ def tile_dygcn_pa_t_kernel(tc, A, x, out):
             right_grouped = work.tile([P, NODES * PACK], BF16, align_bytes=64)
             right_words = right_grouped[:].rearrange("p (t q s) -> p t q s", t=PACK, s=PACK)
             columns = live["a_hat", b][:].rearrange("p s (u q e) -> p u e q s", u=2, e=2)
-            for t in range(PACK):
-                copy = nc.scalar.copy if t == PACK - 1 else nc.vector.tensor_copy
-                copy(out=right_words[:, t, :, :], in_=columns[:, t // 2, t % 2, :, :])
+            for u in range(2):
+                nc.gpsimd.tensor_scalar(
+                    out=right_words[:, 2 * u : 2 * u + 2, :, :],
+                    in0=columns[:, u, :, :, :],
+                    scalar1=1.0,
+                    scalar2=0.0,
+                    op0=ALU.mult,
+                    op1=ALU.add,
+                )
             live["right_grouped", b] = right_grouped
 
         def flip(b):
@@ -146,10 +155,11 @@ def tile_dygcn_pa_t_kernel(tc, A, x, out):
 
         def regroup_x(b):
             x_grouped = work.tile([P, FEATS * PACK], BF16, align_bytes=64)
-            nc.scalar.copy(
-                out=x_grouped[:].rearrange("p (f s) -> p f s", s=PACK),
-                in_=live["x_raw", b][:].rearrange("p s f -> p f s"),
-            )
+            x_words = x_grouped[:].rearrange("p (f s) -> p f s", s=PACK)
+            x_columns = live["x_raw", b][:].rearrange("p s f -> p f s")
+            half = FEATS // 2
+            nc.vector.tensor_copy(out=x_words[:, :half, :], in_=x_columns[:, :half, :])
+            nc.scalar.copy(out=x_words[:, half:, :], in_=x_columns[:, half:, :])
             live["x_grouped", b] = x_grouped
 
         def square(b, c):
@@ -212,23 +222,27 @@ def tile_dygcn_pa_t_kernel(tc, A, x, out):
         with tc.manual_schedule():
             for b in range(LOADS_AHEAD):
                 load(b)
-            for i in range(-2, GRAPHS + 1):
-                front, middle, back, last = i + 2, i + 1, i, i - 1
-                if front + LOADS_AHEAD < GRAPHS:
-                    load(front + LOADS_AHEAD)
+            for i in range(-3, GRAPHS + 1):
+                lead, front, middle, back, last = i + 3, i + 2, i + 1, i, i - 1
+                if lead + LOADS_AHEAD < GRAPHS:
+                    load(lead + LOADS_AHEAD)
+                if 0 <= front < GRAPHS:
+                    add_identity(front)
+                    inverse_root(front)
                 if 0 <= last:
                     times_x(last, "t2")
                 if 0 <= middle < GRAPHS:
                     scale(middle)
-                if front < GRAPHS:
-                    positive_part(front)
                 if 0 <= back < GRAPHS:
                     for c in range(PACK - 1):
                         square(back, c)
                 if 0 <= last:
                     store(last, 1)
+                if lead < GRAPHS:
+                    positive_part(lead)
                 if 0 <= middle < GRAPHS:
                     flip(middle)
+                    regroup_right(middle)
                 if 0 <= back < GRAPHS:
                     for c in range(PACK - 1):
                         chebyshev(back, c)
@@ -236,20 +250,17 @@ def tile_dygcn_pa_t_kernel(tc, A, x, out):
                     chebyshev(back, PACK - 1)
                 if 0 <= middle < GRAPHS:
                     regroup_left(middle)
-                if front < GRAPHS:
-                    inverse_root(front)
                 if 0 <= back < GRAPHS:
                     times_x(back, "left")
-                if front < GRAPHS:
+                if 0 <= front < GRAPHS:
                     spread_r(front)
-                if 0 <= middle < GRAPHS:
-                    regroup_right(middle)
                 if 0 <= back < GRAPHS:
                     store(back, 0)
+                if 0 <= front < GRAPHS:
+                    regroup_x(front)
+                if 0 <= back < GRAPHS:
                     quantise_as(back, "t2", NODES)
                 if 0 <= middle < GRAPHS:
                     quantise_as(middle, "x", FEATS)
                     quantise_as(middle, "left", NODES)
                     quantise_as(middle, "right", NODES)
-                if front < GRAPHS:
-                    regroup_x(front)

@@ -17,6 +17,7 @@ FEATS = 256
 P = 128
 PACK = 4
 
+RIGHT_QUARTERS_ON_VECTOR = 2
 LOADS_AHEAD = 4
 
 FLOPS = GRAPHS * 2 * (NODES * NODES * NODES + 2 * NODES * NODES * FEATS)
@@ -28,6 +29,10 @@ def rows_by_node(dram):
 
 def slots_by_node(tile):
     return tile[:].rearrange("p (u e) w -> p u (e w)", u=2)
+
+
+def in_runs(view):
+    return view.rearrange("p (c i) s -> p c s i", i=4)
 
 
 def quantise(nc, pool, grouped, width, name):
@@ -42,9 +47,8 @@ def tile_dygcn_pa_t_kernel(tc, A, x, out):
     with ExitStack() as stack:
         const = stack.enter_context(tc.tile_pool(name="const", bufs=1))
         loads = stack.enter_context(tc.tile_pool(name="loads", bufs=LOADS_AHEAD + 2))
-        early = stack.enter_context(tc.tile_pool(name="early", bufs=3))
         work = stack.enter_context(tc.tile_pool(name="work", bufs=2))
-        small = stack.enter_context(tc.tile_pool(name="small", bufs=4))
+        small = stack.enter_context(tc.tile_pool(name="small", bufs=3))
         mx = stack.enter_context(tc.tile_pool(name="mx", bufs=3))
         results = stack.enter_context(tc.tile_pool(name="results", bufs=4))
         ps_row = stack.enter_context(tc.psum_pool(name="ps_row", bufs=1))
@@ -63,7 +67,8 @@ def tile_dygcn_pa_t_kernel(tc, A, x, out):
 
         def load(b):
             a_raw = loads.tile([P, PACK, NODES], BF16)
-            nc.sync.dma_start(out=slots_by_node(a_raw), in_=rows_by_node(A[b]))
+            for u in range(2):
+                nc.sync.dma_start(out=slots_by_node(a_raw)[:, u, :], in_=rows_by_node(A[b])[:, u, :])
             x_raw = loads.tile([P, PACK, FEATS], BF16)
             nc.sync.dma_start(out=slots_by_node(x_raw), in_=rows_by_node(x[b]))
             live["a_raw", b] = a_raw
@@ -71,29 +76,23 @@ def tile_dygcn_pa_t_kernel(tc, A, x, out):
 
         def positive_part(b):
             a_raw = live["a_raw", b]
-            pos = early.tile([P, PACK, NODES], F32)
+            pos = work.tile([P, PACK, NODES], F32)
             rowsum = small.tile([P, PACK], F32)
             for t in range(PACK):
                 nc.scalar.activation(
                     out=pos[:, t, :], in_=a_raw[:, t, :], func=ACT.Relu, accum_out=rowsum[:, t : t + 1]
                 )
-            live["pos", b] = pos
-            live["rowsum", b] = rowsum
-
-        def add_identity(b):
             for t in range(PACK):
-                diag = live["pos", b][:, t, :].rearrange("p (u q e) -> p u q e", u=2, e=2)[:, t // 2, :, t % 2]
+                diag = pos[:, t, :].rearrange("p (u q e) -> p u q e", u=2, e=2)[:, t // 2, :, t % 2]
                 nc.gpsimd.tensor_tensor(out=diag, in0=diag, in1=ident_f32[:], op=ALU.add)
+            root_deg = small.tile([P, PACK], F32)
+            nc.scalar.activation(out=root_deg[:], in_=rowsum[:], func=ACT.Sqrt, bias=1.0)
+            live["pos", b] = pos
+            live["root_deg", b] = root_deg
 
         def inverse_root(b):
-            deg = small.tile([P, PACK], F32)
-            nc.vector.tensor_scalar(
-                out=deg[:], in0=live["rowsum", b][:], scalar1=1.0, scalar2=1e-6, op0=ALU.add, op1=ALU.max
-            )
-            inv_deg = small.tile([P, PACK], F32)
-            nc.vector.reciprocal(out=inv_deg[:], in_=deg[:])
             r = small.tile([P, PACK], F32)
-            nc.scalar.activation(out=r[:], in_=inv_deg[:], func=ACT.Sqrt)
+            nc.vector.reciprocal(out=r[:], in_=live["root_deg", b][:])
             live["r", b] = r
 
         def spread_r(b):
@@ -124,15 +123,9 @@ def tile_dygcn_pa_t_kernel(tc, A, x, out):
             right_grouped = work.tile([P, NODES * PACK], BF16, align_bytes=64)
             right_words = right_grouped[:].rearrange("p (t q s) -> p t q s", t=PACK, s=PACK)
             columns = live["a_hat", b][:].rearrange("p s (u q e) -> p u e q s", u=2, e=2)
-            for u in range(2):
-                nc.gpsimd.tensor_scalar(
-                    out=right_words[:, 2 * u : 2 * u + 2, :, :],
-                    in0=columns[:, u, :, :, :],
-                    scalar1=1.0,
-                    scalar2=0.0,
-                    op0=ALU.mult,
-                    op1=ALU.add,
-                )
+            for t in range(PACK):
+                copy = nc.vector.tensor_copy if t < RIGHT_QUARTERS_ON_VECTOR else nc.scalar.copy
+                copy(out=in_runs(right_words[:, t, :, :]), in_=in_runs(columns[:, t // 2, t % 2, :, :]))
             live["right_grouped", b] = right_grouped
 
         def flip(b):
@@ -155,11 +148,10 @@ def tile_dygcn_pa_t_kernel(tc, A, x, out):
 
         def regroup_x(b):
             x_grouped = work.tile([P, FEATS * PACK], BF16, align_bytes=64)
-            x_words = x_grouped[:].rearrange("p (f s) -> p f s", s=PACK)
-            x_columns = live["x_raw", b][:].rearrange("p s f -> p f s")
-            half = FEATS // 2
-            nc.vector.tensor_copy(out=x_words[:, :half, :], in_=x_columns[:, :half, :])
-            nc.scalar.copy(out=x_words[:, half:, :], in_=x_columns[:, half:, :])
+            nc.scalar.copy(
+                out=in_runs(x_grouped[:].rearrange("p (f s) -> p f s", s=PACK)),
+                in_=in_runs(live["x_raw", b][:].rearrange("p s f -> p f s")),
+            )
             live["x_grouped", b] = x_grouped
 
         def square(b, c):
@@ -214,7 +206,7 @@ def tile_dygcn_pa_t_kernel(tc, A, x, out):
             result = results.tile([P, PACK, FEATS], F32)
             for h in range(2):
                 nc.scalar.copy(out=result[:, 2 * h : 2 * h + 2, :], in_=live["acc", b, h][:])
-            nc.sync.dma_start(out=rows_by_node(out[b, which]), in_=slots_by_node(result))
+                nc.sync.dma_start(out=rows_by_node(out[b, which])[:, h, :], in_=slots_by_node(result)[:, h, :])
 
         def quantise_as(b, name, width):
             live[name, b] = quantise(nc, mx, live[name + "_grouped", b][:], width, name)
@@ -222,27 +214,23 @@ def tile_dygcn_pa_t_kernel(tc, A, x, out):
         with tc.manual_schedule():
             for b in range(LOADS_AHEAD):
                 load(b)
-            for i in range(-3, GRAPHS + 1):
-                lead, front, middle, back, last = i + 3, i + 2, i + 1, i, i - 1
-                if lead + LOADS_AHEAD < GRAPHS:
-                    load(lead + LOADS_AHEAD)
-                if 0 <= front < GRAPHS:
-                    add_identity(front)
-                    inverse_root(front)
+            for i in range(-2, GRAPHS + 1):
+                front, middle, back, last = i + 2, i + 1, i, i - 1
+                if front + LOADS_AHEAD < GRAPHS:
+                    load(front + LOADS_AHEAD)
                 if 0 <= last:
                     times_x(last, "t2")
                 if 0 <= middle < GRAPHS:
                     scale(middle)
+                if front < GRAPHS:
+                    positive_part(front)
                 if 0 <= back < GRAPHS:
                     for c in range(PACK - 1):
                         square(back, c)
                 if 0 <= last:
                     store(last, 1)
-                if lead < GRAPHS:
-                    positive_part(lead)
                 if 0 <= middle < GRAPHS:
                     flip(middle)
-                    regroup_right(middle)
                 if 0 <= back < GRAPHS:
                     for c in range(PACK - 1):
                         chebyshev(back, c)
@@ -250,17 +238,20 @@ def tile_dygcn_pa_t_kernel(tc, A, x, out):
                     chebyshev(back, PACK - 1)
                 if 0 <= middle < GRAPHS:
                     regroup_left(middle)
+                if front < GRAPHS:
+                    inverse_root(front)
                 if 0 <= back < GRAPHS:
                     times_x(back, "left")
-                if 0 <= front < GRAPHS:
+                if front < GRAPHS:
                     spread_r(front)
+                if 0 <= middle < GRAPHS:
+                    regroup_right(middle)
                 if 0 <= back < GRAPHS:
                     store(back, 0)
-                if 0 <= front < GRAPHS:
-                    regroup_x(front)
-                if 0 <= back < GRAPHS:
                     quantise_as(back, "t2", NODES)
                 if 0 <= middle < GRAPHS:
                     quantise_as(middle, "x", FEATS)
                     quantise_as(middle, "left", NODES)
                     quantise_as(middle, "right", NODES)
+                if front < GRAPHS:
+                    regroup_x(front)

from contextlib import ExitStack

import concourse.mybir as mybir
from concourse.masks import make_identity

F32 = mybir.dt.float32
BF16 = mybir.dt.bfloat16
U32 = mybir.dt.uint32
U8 = mybir.dt.uint8
FP8X4 = mybir.dt.float8_e4m3fn_x4
ALU = mybir.AluOpType
ACT = mybir.ActivationFunctionType

GRAPHS = 16
NODES = 512
FEATS = 256
P = 128
PACK = 4

RIGHT_QUARTERS_ON_VECTOR = 2
LOADS_AHEAD = 4

FLOPS = GRAPHS * 2 * (NODES * NODES * NODES + 2 * NODES * NODES * FEATS)


def rows_by_node(dram):
    return dram.rearrange("(u p e) w -> p u (e w)", u=2, e=2)


def slots_by_node(tile):
    return tile[:].rearrange("p (u e) w -> p u (e w)", u=2)


def in_runs(view):
    return view.rearrange("p (c i) s -> p c s i", i=4)


def quantise(nc, pool, grouped, width, name):
    codes = pool.tile([P, width], U32, align_bytes=64, name=name + "_codes")
    scales = pool.tile([P, width], U8, align_bytes=64, name=name + "_scales")
    nc.vector.quantize_mx(out=codes[:].bitcast(FP8X4), scales=scales[:], in_=grouped)
    return codes, scales


def tile_dygcn_pa_t_kernel(tc, A, x, out):
    nc = tc.nc
    with ExitStack() as stack:
        const = stack.enter_context(tc.tile_pool(name="const", bufs=1))
        loads = stack.enter_context(tc.tile_pool(name="loads", bufs=LOADS_AHEAD + 2))
        work = stack.enter_context(tc.tile_pool(name="work", bufs=2))
        small = stack.enter_context(tc.tile_pool(name="small", bufs=3))
        mx = stack.enter_context(tc.tile_pool(name="mx", bufs=3))
        results = stack.enter_context(tc.tile_pool(name="results", bufs=4))
        ps_row = stack.enter_context(tc.psum_pool(name="ps_row", bufs=1))
        ps_tr = stack.enter_context(tc.psum_pool(name="ps_tr", bufs=2))
        ps_t2 = stack.enter_context(tc.psum_pool(name="ps_t2", bufs=3))
        ps_out = stack.enter_context(tc.psum_pool(name="ps_out", bufs=2))

        ident_f32 = const.tile([P, P], F32)
        make_identity(nc, ident_f32[:])
        eye_t2 = const.tile([P, PACK, P, PACK], BF16)
        nc.vector.memset(eye_t2[:], 0.0)
        for c in range(PACK):
            nc.vector.tensor_copy(out=eye_t2[:, c, :, c], in_=ident_f32[:])

        live = {}

        def load(b):
            a_raw = loads.tile([P, PACK, NODES], BF16)
            for u in range(2):
                nc.sync.dma_start(out=slots_by_node(a_raw)[:, u, :], in_=rows_by_node(A[b])[:, u, :])
            x_raw = loads.tile([P, PACK, FEATS], BF16)
            nc.sync.dma_start(out=slots_by_node(x_raw), in_=rows_by_node(x[b]))
            live["a_raw", b] = a_raw
            live["x_raw", b] = x_raw

        def positive_part(b):
            a_raw = live["a_raw", b]
            pos = work.tile([P, PACK, NODES], F32)
            rowsum = small.tile([P, PACK], F32)
            for t in range(PACK):
                nc.scalar.activation(
                    out=pos[:, t, :], in_=a_raw[:, t, :], func=ACT.Relu, accum_out=rowsum[:, t : t + 1]
                )
            for t in range(PACK):
                diag = pos[:, t, :].rearrange("p (u q e) -> p u q e", u=2, e=2)[:, t // 2, :, t % 2]
                nc.gpsimd.tensor_tensor(out=diag, in0=diag, in1=ident_f32[:], op=ALU.add)
            root_deg = small.tile([P, PACK], F32)
            nc.scalar.activation(out=root_deg[:], in_=rowsum[:], func=ACT.Sqrt, bias=1.0)
            live["pos", b] = pos
            live["root_deg", b] = root_deg

        def inverse_root(b):
            r = small.tile([P, PACK], F32)
            nc.vector.reciprocal(out=r[:], in_=live["root_deg", b][:])
            live["r", b] = r

        def spread_r(b):
            r = live["r", b]
            r_row = ps_row.tile([P, NODES], F32)
            for t in range(PACK):
                nc.tensor.transpose(
                    r_row[:].rearrange("p (u q e) -> p u q e", u=2, e=2)[:, t // 2, :, t % 2],
                    r[:, t : t + 1].to_broadcast([P, P]),
                    ident_f32[:],
                )
            live["r_row", b] = r_row

        def scale(b):
            a_hat = work.tile([P, PACK, NODES], BF16)
            for t in range(PACK):
                nc.vector.scalar_tensor_tensor(
                    out=a_hat[:, t, :],
                    in0=live["pos", b][:, t, :],
                    scalar=live["r", b][:, t : t + 1],
                    in1=live["r_row", b][:],
                    op0=ALU.mult,
                    op1=ALU.mult,
                )
            live["a_hat", b] = a_hat

        def regroup_right(b):
            right_grouped = work.tile([P, NODES * PACK], BF16, align_bytes=64)
            right_words = right_grouped[:].rearrange("p (t q s) -> p t q s", t=PACK, s=PACK)
            columns = live["a_hat", b][:].rearrange("p s (u q e) -> p u e q s", u=2, e=2)
            for t in range(PACK):
                copy = nc.vector.tensor_copy if t < RIGHT_QUARTERS_ON_VECTOR else nc.scalar.copy
                copy(out=in_runs(right_words[:, t, :, :]), in_=in_runs(columns[:, t // 2, t % 2, :, :]))
            live["right_grouped", b] = right_grouped

        def flip(b):
            for h in range(2):
                flipped = ps_tr.tile([P, 2, 2, P], F32)
                for c in range(2):
                    row_words = live["a_hat", b][:, 2 * h + c, :].bitcast(F32)
                    for u in range(2):
                        nc.tensor.transpose(flipped[:, c, u, :], row_words[:, u * P : (u + 1) * P], ident_f32[:])
                live["flipped", b, h] = flipped

        def regroup_left(b):
            left_grouped = work.tile([P, NODES * PACK], BF16, align_bytes=64)
            left_words = left_grouped[:].bitcast(F32).rearrange("p (h c n u) -> p h c n u", h=2, c=2, u=2)
            for h in range(2):
                nc.scalar.copy(
                    out=left_words[:, h, :, :, :], in_=live["flipped", b, h][:].rearrange("p c u n -> p c n u")
                )
            live["left_grouped", b] = left_grouped

        def regroup_x(b):
            x_grouped = work.tile([P, FEATS * PACK], BF16, align_bytes=64)
            nc.scalar.copy(
                out=in_runs(x_grouped[:].rearrange("p (f s) -> p f s", s=PACK)),
                in_=in_runs(live["x_raw", b][:].rearrange("p s f -> p f s")),
            )
            live["x_grouped", b] = x_grouped

        def square(b, c):
            right_codes, right_scales = live["right", b]
            left_codes, left_scales = live["left", b]
            n_cols = slice(c * P, (c + 1) * P)
            squared = ps_t2.tile([P, PACK, P], F32)
            for t in range(PACK):
                j_cols = slice(t * P, (t + 1) * P)
                nc.tensor.matmul_mx(
                    out=squared[:, t, :],
                    lhsT=right_codes[:, j_cols].bitcast(FP8X4),
                    lhsT_scale=right_scales[:, j_cols],
                    rhs=left_codes[:, n_cols].bitcast(FP8X4),
                    rhs_scale=left_scales[:, n_cols],
                    start=True,
                    stop=True,
                )
            live["squared", b, c] = squared

        def chebyshev(b, c):
            if c == 0:
                live["t2_grouped", b] = work.tile([P, NODES * PACK], BF16, align_bytes=64, name="t2_grouped")
            nc.vector.scalar_tensor_tensor(
                out=live["t2_grouped", b][:].rearrange("p (c n t) -> p c n t", c=PACK, t=PACK)[:, c, :, :],
                in0=live["squared", b, c][:].rearrange("p t n -> p n t"),
                scalar=2.0,
                in1=eye_t2[:, c, :, :],
                op0=ALU.mult,
                op1=ALU.subtract,
            )

        def times_x(b, name):
            codes, scales = live[name, b]
            x_codes, x_scales = live["x", b]
            for h in range(2):
                acc = ps_out.tile([P, 2, FEATS], F32)
                for c in range(2):
                    n_cols = slice((2 * h + c) * P, (2 * h + c + 1) * P)
                    nc.tensor.matmul_mx(
                        out=acc[:, c, :],
                        lhsT=codes[:, n_cols].bitcast(FP8X4),
                        lhsT_scale=scales[:, n_cols],
                        rhs=x_codes[:].bitcast(FP8X4),
                        rhs_scale=x_scales[:],
                        start=True,
                        stop=True,
                    )
                live["acc", b, h] = acc

        def store(b, which):
            result = results.tile([P, PACK, FEATS], F32)
            for h in range(2):
                nc.scalar.copy(out=result[:, 2 * h : 2 * h + 2, :], in_=live["acc", b, h][:])
                nc.sync.dma_start(out=rows_by_node(out[b, which])[:, h, :], in_=slots_by_node(result)[:, h, :])

        def quantise_as(b, name, width):
            live[name, b] = quantise(nc, mx, live[name + "_grouped", b][:], width, name)

        with tc.manual_schedule():
            for b in range(LOADS_AHEAD):
                load(b)
            for i in range(-2, GRAPHS + 1):
                front, middle, back, last = i + 2, i + 1, i, i - 1
                if front + LOADS_AHEAD < GRAPHS:
                    load(front + LOADS_AHEAD)
                if 0 <= last:
                    times_x(last, "t2")
                if 0 <= middle < GRAPHS:
                    scale(middle)
                if front < GRAPHS:
                    positive_part(front)
                if 0 <= back < GRAPHS:
                    for c in range(PACK - 1):
                        square(back, c)
                if 0 <= last:
                    store(last, 1)
                if 0 <= middle < GRAPHS:
                    flip(middle)
                if 0 <= back < GRAPHS:
                    for c in range(PACK - 1):
                        chebyshev(back, c)
                    square(back, PACK - 1)
                    chebyshev(back, PACK - 1)
                if 0 <= middle < GRAPHS:
                    regroup_left(middle)
                if front < GRAPHS:
                    inverse_root(front)
                if 0 <= back < GRAPHS:
                    times_x(back, "left")
                if front < GRAPHS:
                    spread_r(front)
                if 0 <= middle < GRAPHS:
                    regroup_right(middle)
                if 0 <= back < GRAPHS:
                    store(back, 0)
                    quantise_as(back, "t2", NODES)
                if 0 <= middle < GRAPHS:
                    quantise_as(middle, "x", FEATS)
                    quantise_as(middle, "left", NODES)
                    quantise_as(middle, "right", NODES)
                if front < GRAPHS:
                    regroup_x(front)
